import numpy as np
import ml_dtypes


def mxq(x, axis, fmt="e4m3"):
    dtype, down = {"e4m3": (ml_dtypes.float8_e4m3fn, 7), "e5m2": (ml_dtypes.float8_e5m2, 14)}[fmt]
    v = np.moveaxis(np.asarray(x, np.float32).astype(ml_dtypes.bfloat16).astype(np.float64), axis, -1)
    blocks = v.reshape(v.shape[:-1] + (-1, 32))
    amax = np.abs(blocks).max(-1, keepdims=True)
    byte = np.maximum(np.where(amax > 0, np.frexp(amax)[1] - 1 + 127, 0) - down, 1)
    scale = np.exp2(byte - 127.0)
    codes = (blocks / scale).astype(np.float32).astype(dtype).astype(np.float64)
    return np.moveaxis((codes * scale).reshape(v.shape), -1, axis)


WIDE = False


def mx_kscale(k):
    if not WIDE:
        return np.ones(k)
    levels = np.array([10, -10, 5, -5, 0])
    if k % 512:
        return np.exp2(np.random.permutation(np.resize(levels, k // 32))).repeat(32)
    a = np.empty((k // 512, 16))
    for p in range(k // 512):
        a[p, :8] = np.random.permutation(np.resize(levels, 8))
        for g in range(8):
            far = levels[np.abs(levels - a[p, g]) >= 10]
            a[p, g + 8] = far[np.random.randint(len(far))]
    return np.exp2(a.ravel()).repeat(32)


BF16 = ml_dtypes.bfloat16


def bf(x):
    return np.asarray(x, np.float32).astype(BF16)


def f64(x):
    return np.asarray(x).astype(np.float64)


B, S, E, H, DH, ROT, MP = 2, 512, 1024, 8, 128, 32, 4
HD = H * DH
LOC = HD // MP


def rope_sincos():
    inv_freq = 1.0 / (10000.0 ** (np.arange(0, ROT, 2) / ROT))
    ang = np.arange(S)[:, None] * inv_freq[None, :]
    return np.sin(ang), np.cos(ang)


def apply_rope(x, sin, cos):
    sin2 = np.repeat(sin, 2, axis=-1)[None, :, None, :]
    cos2 = np.repeat(cos, 2, axis=-1)[None, :, None, :]
    x1 = x[..., ::2]
    x2 = x[..., 1::2]
    rot = np.stack((-x2, x1), axis=-1).reshape(x.shape)
    return x * cos2 + rot * sin2


def setup_inputs():
    s = mx_kscale(E)
    return {"hidden_states": bf(np.random.standard_normal((B, S, E)) * s),
            "W_qkv": bf(np.random.standard_normal((3 * HD, E)) / np.sqrt(E) / s[None, :])}


def reference(hidden_states, W_qkv):
    qkv = mxq(f64(hidden_states), 2, "e4m3") @ mxq(f64(W_qkv).T, 0, "e4m3")
    qkv = qkv.reshape(B, S, MP, 3 * LOC)
    q, k, v = np.split(qkv, 3, axis=-1)
    q = q.reshape(B, S, H, DH)
    k = k.reshape(B, S, H, DH)
    v = v.reshape(B, S, H, DH)
    sin, cos = rope_sincos()
    q = np.concatenate([apply_rope(q[..., :ROT], sin, cos), q[..., ROT:]], axis=-1)
    k = np.concatenate([apply_rope(k[..., :ROT], sin, cos), k[..., ROT:]], axis=-1)
    return q, k, v

@@ -1,0 +1,282 @@
+import math
+from contextlib import ExitStack
+
+import concourse.mybir as mybir
+from concourse.masks import make_identity
+
+F32 = mybir.dt.float32
+BF16 = mybir.dt.bfloat16
+I32 = mybir.dt.int32
+U32 = mybir.dt.uint32
+U8 = mybir.dt.uint8
+FP8X4 = mybir.dt.float8_e4m3fn_x4
+ALU = mybir.AluOpType
+ACT = mybir.ActivationFunctionType
+
+P = 128
+SEQ = 512
+TOKENS = 2 * SEQ
+TOKEN_TILES = TOKENS // P
+TILE_PAIRS = TOKEN_TILES // 2
+E = 1024
+PASSES = E // 512
+HEADS = 8
+DH = 128
+ROT = 32
+PAIRS = ROT // 2
+WIDTH = HEADS * DH
+GROUPS = 4
+GROUP_ROWS = WIDTH // GROUPS
+HALVES = 2
+HALF = WIDTH // HALVES
+Q, K, V = 0, 1, 2
+PSUM_BANKS = 8
+
+FLOPS = 2 * TOKENS * E * 3 * WIDTH
+
+ROUND_MAGIC = 1.5 * 2.0**23
+TURN_HI = 6.28125
+TURN_LO = 2.0 * math.pi - TURN_HI
+
+
+def build_rope_tables(nc, pool):
+    token = pool.tile([P, TOKEN_TILES], I32, name="token")
+    nc.gpsimd.iota(token[:], pattern=[[1, TOKEN_TILES]], base=0, channel_multiplier=TOKEN_TILES)
+    position_i = pool.tile([P, TOKEN_TILES], I32, name="position_i")
+    nc.vector.tensor_single_scalar(out=position_i[:], in_=token[:], scalar=SEQ - 1, op=ALU.bitwise_and)
+    position = pool.tile([P, TOKEN_TILES], F32, name="position")
+    nc.vector.tensor_copy(out=position[:], in_=position_i[:])
+
+    shape = [P, TOKEN_TILES, PAIRS]
+    angle = pool.tile(shape, F32, name="angle")
+    for j in range(PAIRS):
+        nc.vector.tensor_scalar_mul(
+            out=angle[:, :, j], in0=position[:], scalar1=10000.0 ** (-2.0 * j / ROT)
+        )
+    turns = pool.tile(shape, F32, name="turns")
+    nc.vector.tensor_scalar(
+        out=turns[:], in0=angle[:], scalar1=0.5 / math.pi, scalar2=ROUND_MAGIC,
+        op0=ALU.mult, op1=ALU.add,
+    )
+    nc.vector.tensor_scalar_sub(out=turns[:], in0=turns[:], scalar1=ROUND_MAGIC)
+    partly = pool.tile(shape, F32, name="partly")
+    nc.vector.scalar_tensor_tensor(
+        out=partly[:], in0=turns[:], scalar=-TURN_HI, in1=angle[:], op0=ALU.mult, op1=ALU.add
+    )
+    reduced = pool.tile(shape, F32, name="reduced")
+    nc.vector.scalar_tensor_tensor(
+        out=reduced[:], in0=turns[:], scalar=-TURN_LO, in1=partly[:], op0=ALU.mult, op1=ALU.add
+    )
+    sin_half = pool.tile(shape, F32, name="sin_half")
+    nc.scalar.activation(out=sin_half[:], in_=reduced[:], func=ACT.Sin, scale=0.5)
+    size = pool.tile(shape, F32, name="size")
+    nc.vector.scalar_tensor_tensor(
+        out=size[:], in0=reduced[:], scalar=-1.0, in1=reduced[:], op0=ALU.mult, op1=ALU.max
+    )
+    nc.vector.tensor_scalar(
+        out=size[:], in0=size[:], scalar1=-0.5, scalar2=0.5 * math.pi, op0=ALU.mult, op1=ALU.add
+    )
+    cos_half = pool.tile(shape, F32, name="cos_half")
+    nc.scalar.activation(out=cos_half[:], in_=size[:], func=ACT.Sin)
+
+    table = pool.tile([P, TOKEN_TILES, 2, ROT], F32, name="table")
+    entry = table[:].rearrange("p t r (j c) -> p t r j c", c=2)
+    nc.vector.scalar_tensor_tensor(
+        out=entry[:, :, 1, :, 0], in0=sin_half[:], scalar=2.0, in1=cos_half[:],
+        op0=ALU.mult, op1=ALU.mult,
+    )
+    nc.vector.scalar_tensor_tensor(
+        out=entry[:, :, 0, :, 1], in0=sin_half[:], scalar=-2.0, in1=cos_half[:],
+        op0=ALU.mult, op1=ALU.mult,
+    )
+    cos_less_1 = pool.tile(shape, F32, name="cos_less_1")
+    nc.vector.scalar_tensor_tensor(
+        out=cos_less_1[:], in0=sin_half[:], scalar=-2.0, in1=sin_half[:],
+        op0=ALU.mult, op1=ALU.mult,
+    )
+    nc.vector.tensor_scalar_add(out=entry[:, :, 0, :, 0], in0=cos_less_1[:], scalar1=1.0)
+    nc.vector.tensor_scalar_add(out=entry[:, :, 1, :, 1], in0=cos_less_1[:], scalar1=1.0)
+    return table
+
+
+def tile_progenattention_pa_kernel(tc, hidden_states, W_qkv, out_0, out_1, out_2):
+    nc = tc.nc
+
+    x_dram = hidden_states.rearrange("b s k -> (b s) k").rearrange(
+        "(p t) k -> p t k", t=TOKEN_TILES
+    )
+    out_dram = [
+        out.rearrange("b s h d -> (b s) (h d)").rearrange("(p t) c -> p t c", t=TOKEN_TILES)
+        for out in (out_0, out_1, out_2)
+    ]
+    w_dram = W_qkv.rearrange("(g s p i) k -> s g p (i k)", g=GROUPS, s=3, p=P, i=2)
+
+    with ExitStack() as ctx:
+        consts = ctx.enter_context(tc.tile_pool(name="consts", bufs=1))
+        raw = ctx.enter_context(tc.tile_pool(name="raw", bufs=1))
+        keep = ctx.enter_context(tc.tile_pool(name="keep", bufs=1))
+        stage = ctx.enter_context(tc.tile_pool(name="stage", bufs=4))
+        results = ctx.enter_context(tc.tile_pool(name="results", bufs=TOKEN_TILES + 4))
+        psum = ctx.enter_context(tc.psum_pool(name="psum", bufs=PSUM_BANKS))
+        ctx.enter_context(tc.manual_schedule())
+
+        x_pairs = list(range(TILE_PAIRS))
+        w_halves = [(s, a) for s in (V, Q, K) for a in range(HALVES)]
+        x_raw = {}
+        w_raw = {}
+
+        def load_x(n):
+            x_raw[n] = raw.tile([P, 2, E], BF16, name="x_raw_%d" % n)
+            nc.sync.dma_start(out=x_raw[n][:], in_=x_dram[:, 2 * n : 2 * n + 2, :])
+
+        def load_w(s, a):
+            for g in (2 * a, 2 * a + 1):
+                w_raw[(s, g)] = raw.tile([P, 2 * E], BF16, name="w_raw_%d_%d" % (s, g))
+                nc.sync.dma_start(out=w_raw[(s, g)][:], in_=w_dram[s, g, :, :])
+
+        load_x(x_pairs[0])
+        load_w(*w_halves[0])
+        for n in x_pairs[1:]:
+            load_x(n)
+        for s, a in w_halves[1:]:
+            load_w(s, a)
+
+        identity = consts.tile([P, P], F32, name="identity")
+        make_identity(nc, identity[:])
+        table = build_rope_tables(nc, consts)
+
+        def leave_psum(n, out, in_):
+            if n % 2 == 0:
+                nc.vector.tensor_copy(out=out, in_=in_)
+            else:
+                nc.scalar.copy(out=out, in_=in_)
+
+        x_codes = keep.tile([P, TOKEN_TILES * PASSES * P], U32, name="x_codes", align_bytes=64)
+        x_scales = keep.tile([P, TOKEN_TILES * PASSES * P], U8, name="x_scales", align_bytes=64)
+
+        def prepare_x(n):
+            x_grouped = stage.tile([P, 2, PASSES * P * 4], BF16, name="x_grouped", align_bytes=64)
+            for i in range(2):
+                words = x_raw[n][:, i, :].bitcast(F32)
+                x_bank = psum.tile([P, 4, P], F32, name="x_bank", tag="bank")
+                for b in range(4):
+                    first = (b // 2) * 2 * P + b % 2
+                    nc.tensor.transpose(
+                        out=x_bank[:, b, :],
+                        in_=words[:, first : (b // 2 + 1) * 2 * P : 2],
+                        identity=identity[:],
+                    )
+                leave_psum(
+                    i,
+                    x_grouped[:, i, :].bitcast(F32).rearrange("q (c p u) -> q c p u", c=PASSES, u=2),
+                    x_bank[:].rearrange("q (c u) p -> q c p u", u=2),
+                )
+            both_tiles = slice(2 * n * PASSES * P, 2 * (n + 1) * PASSES * P)
+            nc.vector.quantize_mx(
+                out=x_codes[:, both_tiles].bitcast(FP8X4),
+                scales=x_scales[:, both_tiles],
+                in_=x_grouped[:].rearrange("q i k -> q (i k)"),
+            )
+
+        w_codes = {}
+        w_scales = {}
+        for s in (V, Q, K):
+            w_codes[s] = keep.tile(
+                [P, HALVES, PASSES, HALF], U32, name="w_codes_%d" % s, align_bytes=64
+            )
+            w_scales[s] = keep.tile(
+                [P, HALVES, PASSES, HALF], U8, name="w_scales_%d" % s, align_bytes=64
+            )
+
+        def prepare_w(s, a):
+            w_grouped = stage.tile([P, PASSES, HALF * 4], BF16, name="w_grouped", align_bytes=64)
+            for g in range(2):
+                words = w_raw[(s, 2 * a + g)][:].bitcast(F32)
+                for c in range(PASSES):
+                    w_bank = psum.tile([P, 4, P], F32, name="w_bank", tag="bank")
+                    for i in range(2):
+                        for u in range(2):
+                            first = (4 * i + 2 * c) * P
+                            nc.tensor.transpose(
+                                out=w_bank[:, 2 * i + u, :],
+                                in_=words[:, first + u : first + 2 * P : 2],
+                                identity=identity[:],
+                            )
+                    group = w_grouped[:, c, g * 4 * GROUP_ROWS : (g + 1) * 4 * GROUP_ROWS]
+                    leave_psum(
+                        g + c,
+                        group.bitcast(F32).rearrange("q (p b) -> q p b", b=4),
+                        w_bank[:].rearrange("q b p -> q p b"),
+                    )
+            for c in range(PASSES):
+                nc.vector.quantize_mx(
+                    out=w_codes[s][:, a, c, :].bitcast(FP8X4),
+                    scales=w_scales[s][:, a, c, :],
+                    in_=w_grouped[:, c, :],
+                )
+
+        def project_half(s, a, t, result):
+            sums = psum.tile([P, HALF], F32, name="sums", tag="bank")
+            for c in range(PASSES):
+                tokens = slice((PASSES * t + c) * P, (PASSES * t + c + 1) * P)
+                nc.tensor.matmul_mx(
+                    out=sums[:],
+                    lhsT=x_codes[:, tokens].bitcast(FP8X4),
+                    lhsT_scale=x_scales[:, tokens],
+                    rhs=w_codes[s][:, a, c, :].bitcast(FP8X4),
+                    rhs_scale=w_scales[s][:, a, c, :],
+                    start=(c == 0),
+                    stop=(c == PASSES - 1),
+                )
+            nc.scalar.copy(out=result[:, a * HALF : (a + 1) * HALF], in_=sums[:])
+
+        def store(s, t, result):
+            nc.sync.dma_start(out=out_dram[s][:, t, :], in_=result[:])
+
+        def rotated_part(result, a):
+            half = result[:, a * HALF : (a + 1) * HALF]
+            return half.rearrange("p (h d) -> p h d", d=DH)[:, :, 0:ROT]
+
+        def rotation_products(result, t, a):
+            shape = [P, 2, HEADS // HALVES, ROT]
+            products = stage.tile(shape, F32, name="products")
+            nc.vector.tensor_tensor(
+                out=products[:],
+                in0=rotated_part(result, a).unsqueeze(1).to_broadcast(shape),
+                in1=table[:, t, :, :].unsqueeze(2).to_broadcast(shape),
+                op=ALU.mult,
+            )
+            return products
+
+        def rotation_sums(result, a, products):
+            terms = products[:].rearrange("p r h (j c) -> p h j r c", c=2)
+            nc.vector.tensor_tensor(
+                out=rotated_part(result, a).rearrange("p h (j r) -> p h j r", r=2),
+                in0=terms[:, :, :, :, 0],
+                in1=terms[:, :, :, :, 1],
+                op=ALU.add,
+            )
+
+        prepare_x(x_pairs[0])
+        prepare_w(*w_halves[0])
+        later = [(prepare_x, (n,)) for n in x_pairs[1:]] + [(prepare_w, h) for h in w_halves[1:]]
+        assert len(later) == HALVES * TILE_PAIRS
+        v_result = [results.tile([P, WIDTH], F32, name="result") for t in range(TOKEN_TILES)]
+        for a in range(HALVES):
+            for n in x_pairs:
+                prepare, piece = later[a * TILE_PAIRS + n]
+                prepare(*piece)
+                for t in (2 * n, 2 * n + 1):
+                    project_half(V, a, t, v_result[t])
+                    if a == HALVES - 1:
+                        store(V, t, v_result[t])
+
+        for s in (Q, K):
+            for t in range(TOKEN_TILES):
+                result = results.tile([P, WIDTH], F32, name="result")
+                for a in range(HALVES):
+                    project_half(s, a, t, result)
+                products = [rotation_products(result, t, a) for a in range(HALVES)]
+                for a in range(HALVES):
+                    rotation_sums(result, a, products[a])
+                store(s, t, result)

@@ -155,7 +155,9 @@ def tile_progenattention_pa_kernel(tc, hidden_states, W_qkv, out_0, out_1, out_2
         x_scales = keep.tile([P, TOKEN_TILES * PASSES * P], U8, name="x_scales", align_bytes=64)
 
         def prepare_x(n):
-            x_grouped = stage.tile([P, 2, PASSES * P * 4], BF16, name="x_grouped", align_bytes=64)
+            x_grouped = stage.tile(
+                [P, 2, PASSES * P * 4], BF16, name="x_grouped", tag="grouped", align_bytes=64
+            )
             for i in range(2):
                 words = x_raw[n][:, i, :].bitcast(F32)
                 x_bank = psum.tile([P, 4, P], F32, name="x_bank", tag="bank")
@@ -188,23 +190,45 @@ def tile_progenattention_pa_kernel(tc, hidden_states, W_qkv, out_0, out_1, out_2
                 [P, HALVES, PASSES, HALF], U8, name="w_scales_%d" % s, align_bytes=64
             )
 
+        w_sorted = {}
+
+        def sort_w(s, a):
+            for g in (2 * a, 2 * a + 1):
+                w_sorted[(s, g)] = stage.tile([P, 2 * E], BF16, name="w_sorted")
+                nc.vector.tensor_copy(
+                    out=w_sorted[(s, g)][:].bitcast(F32).rearrange("q (b u p) -> q b u p", u=2, p=P),
+                    in_=w_raw[(s, g)][:].bitcast(F32).rearrange("q (b p u) -> q b u p", u=2, p=P),
+                )
+
         def prepare_w(s, a):
-            w_grouped = stage.tile([P, PASSES, HALF * 4], BF16, name="w_grouped", align_bytes=64)
+            w_grouped = stage.tile(
+                [P, PASSES, HALF * 4], BF16, name="w_grouped", tag="grouped", align_bytes=64
+            )
+            is_sorted = (s, 2 * a) in w_sorted
             for g in range(2):
-                words = w_raw[(s, 2 * a + g)][:].bitcast(F32)
+                if is_sorted:
+                    words = w_sorted[(s, 2 * a + g)][:].bitcast(F32)
+                else:
+                    words = w_raw[(s, 2 * a + g)][:].bitcast(F32)
                 for c in range(PASSES):
                     w_bank = psum.tile([P, 4, P], F32, name="w_bank", tag="bank")
                     for i in range(2):
                         for u in range(2):
                             first = (4 * i + 2 * c) * P
+                            if is_sorted:
+                                chosen = words[:, first + u * P : first + (u + 1) * P]
+                            else:
+                                chosen = words[:, first + u : first + 2 * P : 2]
                             nc.tensor.transpose(
-                                out=w_bank[:, 2 * i + u, :],
-                                in_=words[:, first + u : first + 2 * P : 2],
-                                identity=identity[:],
+                                out=w_bank[:, 2 * i + u, :], in_=chosen, identity=identity[:]
                             )
                     group = w_grouped[:, c, g * 4 * GROUP_ROWS : (g + 1) * 4 * GROUP_ROWS]
+                    if is_sorted:
+                        engine = 0 if (g, c) == (1, 1) else 1
+                    else:
+                        engine = g + c
                     leave_psum(
-                        g + c,
+                        engine,
                         group.bitcast(F32).rearrange("q (p b) -> q p b", b=4),
                         w_bank[:].rearrange("q b p -> q p b"),
                     )
@@ -228,30 +252,37 @@ def tile_progenattention_pa_kernel(tc, hidden_states, W_qkv, out_0, out_1, out_2
                     start=(c == 0),
                     stop=(c == PASSES - 1),
                 )
+            return sums
+
+        def by_head(columns):
+            return columns.rearrange("p (h d) -> p h d", d=DH)
+
+        def leave_whole(sums, a, result):
             nc.scalar.copy(out=result[:, a * HALF : (a + 1) * HALF], in_=sums[:])
+
+        def leave_unrotated(sums, a, result):
+            nc.scalar.copy(
+                out=by_head(result[:, a * HALF : (a + 1) * HALF])[:, :, ROT:DH],
+                in_=by_head(sums[:])[:, :, ROT:DH],
+            )
 
         def store(s, t, result):
             nc.sync.dma_start(out=out_dram[s][:, t, :], in_=result[:])
 
-        def rotated_part(result, a):
-            half = result[:, a * HALF : (a + 1) * HALF]
-            return half.rearrange("p (h d) -> p h d", d=DH)[:, :, 0:ROT]
-
-        def rotation_products(result, t, a):
-            shape = [P, 2, HEADS // HALVES, ROT]
-            products = stage.tile(shape, F32, name="products")
+        def rotation_products(sums, t, a, products):
+            heads = HEADS // HALVES
+            shape = [P, 2, heads, ROT]
             nc.vector.tensor_tensor(
-                out=products[:],
-                in0=rotated_part(result, a).unsqueeze(1).to_broadcast(shape),
+                out=products[:, :, a * heads : (a + 1) * heads, :],
+                in0=by_head(sums[:])[:, :, 0:ROT].unsqueeze(1).to_broadcast(shape),
                 in1=table[:, t, :, :].unsqueeze(2).to_broadcast(shape),
                 op=ALU.mult,
             )
-            return products
 
-        def rotation_sums(result, a, products):
+        def rotation_sums(result, products):
             terms = products[:].rearrange("p r h (j c) -> p h j r c", c=2)
             nc.vector.tensor_tensor(
-                out=rotated_part(result, a).rearrange("p h (j r) -> p h j r", r=2),
+                out=by_head(result[:])[:, :, 0:ROT].rearrange("p h (j r) -> p h j r", r=2),
                 in0=terms[:, :, :, :, 0],
                 in1=terms[:, :, :, :, 1],
                 op=ALU.add,
@@ -259,24 +290,39 @@ def tile_progenattention_pa_kernel(tc, hidden_states, W_qkv, out_0, out_1, out_2
 
         prepare_x(x_pairs[0])
         prepare_w(*w_halves[0])
-        later = [(prepare_x, (n,)) for n in x_pairs[1:]] + [(prepare_w, h) for h in w_halves[1:]]
+        later = [(prepare_x, (n,), False) for n in x_pairs[1:]]
+        later += [(prepare_w, h, True) for h in w_halves[1:]]
         assert len(later) == HALVES * TILE_PAIRS
         v_result = [results.tile([P, WIDTH], F32, name="result") for t in range(TOKEN_TILES)]
         for a in range(HALVES):
             for n in x_pairs:
-                prepare, piece = later[a * TILE_PAIRS + n]
+                step = a * TILE_PAIRS + n
+                if step + 1 < len(later) and later[step + 1][2]:
+                    sort_w(*later[step + 1][1])
+                prepare, piece, to_sort = later[step]
                 prepare(*piece)
                 for t in (2 * n, 2 * n + 1):
-                    project_half(V, a, t, v_result[t])
+                    leave_whole(project_half(V, a, t, v_result[t]), a, v_result[t])
                     if a == HALVES - 1:
                         store(V, t, v_result[t])
+
+        waiting = []
+
+        def finish_waiting():
+            for s, t, result, products in waiting:
+                rotation_sums(result, products)
+                store(s, t, result)
+            waiting.clear()
 
         for s in (Q, K):
             for t in range(TOKEN_TILES):
                 result = results.tile([P, WIDTH], F32, name="result")
+                products = stage.tile([P, 2, HEADS, ROT], F32, name="products")
                 for a in range(HALVES):
-                    project_half(s, a, t, result)
-                products = [rotation_products(result, t, a) for a in range(HALVES)]
-                for a in range(HALVES):
-                    rotation_sums(result, a, products[a])
-                store(s, t, result)
+                    sums = project_half(s, a, t, result)
+                    leave_unrotated(sums, a, result)
+                    rotation_products(sums, t, a, products)
+                    if a == 0:
+                        finish_waiting()
+                waiting.append((s, t, result, products))
+        finish_waiting()

@@ -116,68 +116,91 @@ def tile_progenattention_pa_kernel(tc, hidden_states, W_qkv, out_0, out_1, out_2
         raw = ctx.enter_context(tc.tile_pool(name="raw", bufs=1))
         keep = ctx.enter_context(tc.tile_pool(name="keep", bufs=1))
         stage = ctx.enter_context(tc.tile_pool(name="stage", bufs=4))
-        results = ctx.enter_context(tc.tile_pool(name="results", bufs=TOKEN_TILES + 4))
+        results = ctx.enter_context(tc.tile_pool(name="results", bufs=12))
         psum = ctx.enter_context(tc.psum_pool(name="psum", bufs=PSUM_BANKS))
         ctx.enter_context(tc.manual_schedule())
 
-        x_pairs = list(range(TILE_PAIRS))
-        w_halves = [(s, a) for s in (V, Q, K) for a in range(HALVES)]
-        x_raw = {}
-        w_raw = {}
+        pieces = {}
 
         def load_x(n):
-            x_raw[n] = raw.tile([P, 2, E], BF16, name="x_raw_%d" % n)
-            nc.sync.dma_start(out=x_raw[n][:], in_=x_dram[:, 2 * n : 2 * n + 2, :])
+            pieces[("x", n)] = raw.tile([P, 2 * E], BF16, name="x_raw_%d" % n)
+            nc.sync.dma_start(
+                out=pieces[("x", n)][:].rearrange("p (i k) -> p i k", i=2),
+                in_=x_dram[:, 2 * n : 2 * n + 2, :],
+            )
 
         def load_w(s, a):
             for g in (2 * a, 2 * a + 1):
-                w_raw[(s, g)] = raw.tile([P, 2 * E], BF16, name="w_raw_%d_%d" % (s, g))
-                nc.sync.dma_start(out=w_raw[(s, g)][:], in_=w_dram[s, g, :, :])
+                pieces[(s, g)] = raw.tile([P, 2 * E], BF16, name="w_raw_%d_%d" % (s, g))
+                nc.sync.dma_start(out=pieces[(s, g)][:], in_=w_dram[s, g, :, :])
 
-        load_x(x_pairs[0])
-        load_w(*w_halves[0])
-        for n in x_pairs[1:]:
+        load_x(0)
+        load_w(V, 0)
+        load_w(V, 1)
+        for n in range(1, TILE_PAIRS):
             load_x(n)
-        for s, a in w_halves[1:]:
-            load_w(s, a)
+        for s in (Q, K):
+            for a in range(HALVES):
+                load_w(s, a)
 
         identity = consts.tile([P, P], F32, name="identity")
         make_identity(nc, identity[:])
         table = build_rope_tables(nc, consts)
 
-        def leave_psum(n, out, in_):
-            if n % 2 == 0:
+        VECTOR, SCALAR = 0, 1
+
+        def leave_psum(engine, out, in_):
+            if engine == VECTOR:
                 nc.vector.tensor_copy(out=out, in_=in_)
             else:
                 nc.scalar.copy(out=out, in_=in_)
 
+        is_sorted = set()
+
+        def sort_piece(key):
+            tidy = stage.tile([P, 2 * E], BF16, name="tidy")
+            nc.vector.tensor_copy(
+                out=tidy[:].bitcast(F32).rearrange("q (b u p) -> q b u p", u=2, p=P),
+                in_=pieces[key][:].bitcast(F32).rearrange("q (b p u) -> q b u p", u=2, p=P),
+            )
+            pieces[key] = tidy
+            is_sorted.add(key)
+
+        def transpose_words(out, key, i, c, u):
+            words = pieces[key][:].bitcast(F32)
+            first = (2 * i + c) * 2 * P
+            if key in is_sorted:
+                chosen = words[:, first + u * P : first + (u + 1) * P]
+            else:
+                chosen = words[:, first + u : first + 2 * P : 2]
+            nc.tensor.transpose(out=out, in_=chosen, identity=identity[:])
+
         x_codes = keep.tile([P, TOKEN_TILES * PASSES * P], U32, name="x_codes", align_bytes=64)
         x_scales = keep.tile([P, TOKEN_TILES * PASSES * P], U8, name="x_scales", align_bytes=64)
+        grouped = {}
 
-        def prepare_x(n):
+        def transpose_x(n):
             x_grouped = stage.tile(
                 [P, 2, PASSES * P * 4], BF16, name="x_grouped", tag="grouped", align_bytes=64
             )
             for i in range(2):
-                words = x_raw[n][:, i, :].bitcast(F32)
                 x_bank = psum.tile([P, 4, P], F32, name="x_bank", tag="bank")
-                for b in range(4):
-                    first = (b // 2) * 2 * P + b % 2
-                    nc.tensor.transpose(
-                        out=x_bank[:, b, :],
-                        in_=words[:, first : (b // 2 + 1) * 2 * P : 2],
-                        identity=identity[:],
-                    )
+                for c in range(PASSES):
+                    for u in range(2):
+                        transpose_words(x_bank[:, 2 * c + u, :], ("x", n), i, c, u)
                 leave_psum(
-                    i,
+                    (VECTOR, SCALAR)[i],
                     x_grouped[:, i, :].bitcast(F32).rearrange("q (c p u) -> q c p u", c=PASSES, u=2),
                     x_bank[:].rearrange("q (c u) p -> q c p u", u=2),
                 )
+            grouped[("x", n)] = x_grouped
+
+        def quantise_x(n):
             both_tiles = slice(2 * n * PASSES * P, 2 * (n + 1) * PASSES * P)
             nc.vector.quantize_mx(
                 out=x_codes[:, both_tiles].bitcast(FP8X4),
                 scales=x_scales[:, both_tiles],
-                in_=x_grouped[:].rearrange("q i k -> q (i k)"),
+                in_=grouped[("x", n)][:].rearrange("q i k -> q (i k)"),
             )
 
         w_codes = {}
@@ -190,56 +213,32 @@ def tile_progenattention_pa_kernel(tc, hidden_states, W_qkv, out_0, out_1, out_2
                 [P, HALVES, PASSES, HALF], U8, name="w_scales_%d" % s, align_bytes=64
             )
 
-        w_sorted = {}
-
-        def sort_w(s, a):
-            for g in (2 * a, 2 * a + 1):
-                w_sorted[(s, g)] = stage.tile([P, 2 * E], BF16, name="w_sorted")
-                nc.vector.tensor_copy(
-                    out=w_sorted[(s, g)][:].bitcast(F32).rearrange("q (b u p) -> q b u p", u=2, p=P),
-                    in_=w_raw[(s, g)][:].bitcast(F32).rearrange("q (b p u) -> q b u p", u=2, p=P),
-                )
-
-        def prepare_w(s, a):
+        def transpose_w(s, a, vector_banks):
             w_grouped = stage.tile(
                 [P, PASSES, HALF * 4], BF16, name="w_grouped", tag="grouped", align_bytes=64
             )
-            is_sorted = (s, 2 * a) in w_sorted
             for g in range(2):
-                if is_sorted:
-                    words = w_sorted[(s, 2 * a + g)][:].bitcast(F32)
-                else:
-                    words = w_raw[(s, 2 * a + g)][:].bitcast(F32)
                 for c in range(PASSES):
                     w_bank = psum.tile([P, 4, P], F32, name="w_bank", tag="bank")
                     for i in range(2):
                         for u in range(2):
-                            first = (4 * i + 2 * c) * P
-                            if is_sorted:
-                                chosen = words[:, first + u * P : first + (u + 1) * P]
-                            else:
-                                chosen = words[:, first + u : first + 2 * P : 2]
-                            nc.tensor.transpose(
-                                out=w_bank[:, 2 * i + u, :], in_=chosen, identity=identity[:]
-                            )
+                            transpose_words(w_bank[:, 2 * i + u, :], (s, 2 * a + g), i, c, u)
                     group = w_grouped[:, c, g * 4 * GROUP_ROWS : (g + 1) * 4 * GROUP_ROWS]
-                    if is_sorted:
-                        engine = 0 if (g, c) == (1, 1) else 1
-                    else:
-                        engine = g + c
                     leave_psum(
-                        engine,
+                        VECTOR if 2 * g + c < vector_banks else SCALAR,
                         group.bitcast(F32).rearrange("q (p b) -> q p b", b=4),
                         w_bank[:].rearrange("q b p -> q p b"),
                     )
-            for c in range(PASSES):
-                nc.vector.quantize_mx(
-                    out=w_codes[s][:, a, c, :].bitcast(FP8X4),
-                    scales=w_scales[s][:, a, c, :],
-                    in_=w_grouped[:, c, :],
-                )
+            grouped[(s, a)] = w_grouped
 
-        def project_half(s, a, t, result):
+        def quantise_w(s, a):
+            nc.vector.quantize_mx(
+                out=w_codes[s][:, a, :, :].rearrange("q c n -> q (c n)").bitcast(FP8X4),
+                scales=w_scales[s][:, a, :, :].rearrange("q c n -> q (c n)"),
+                in_=grouped[(s, a)][:].rearrange("q c k -> q (c k)"),
+            )
+
+        def project_half(s, a, t):
             sums = psum.tile([P, HALF], F32, name="sums", tag="bank")
             for c in range(PASSES):
                 tokens = slice((PASSES * t + c) * P, (PASSES * t + c + 1) * P)
@@ -257,17 +256,18 @@ def tile_progenattention_pa_kernel(tc, hidden_states, W_qkv, out_0, out_1, out_2
         def by_head(columns):
             return columns.rearrange("p (h d) -> p h d", d=DH)
 
-        def leave_whole(sums, a, result):
-            nc.scalar.copy(out=result[:, a * HALF : (a + 1) * HALF], in_=sums[:])
-
-        def leave_unrotated(sums, a, result):
-            nc.scalar.copy(
-                out=by_head(result[:, a * HALF : (a + 1) * HALF])[:, :, ROT:DH],
-                in_=by_head(sums[:])[:, :, ROT:DH],
-            )
-
         def store(s, t, result):
             nc.sync.dma_start(out=out_dram[s][:, t, :], in_=result[:])
+
+        v_result = {}
+
+        def v_half(a, t):
+            if a == 0:
+                v_result[t] = results.tile([P, WIDTH], F32, name="result")
+            sums = project_half(V, a, t)
+            nc.scalar.copy(out=v_result[t][:, a * HALF : (a + 1) * HALF], in_=sums[:])
+            if a == HALVES - 1:
+                store(V, t, v_result[t])
 
         def rotation_products(sums, t, a, products):
             heads = HEADS // HALVES
@@ -288,24 +288,6 @@ def tile_progenattention_pa_kernel(tc, hidden_states, W_qkv, out_0, out_1, out_2
                 op=ALU.add,
             )
 
-        prepare_x(x_pairs[0])
-        prepare_w(*w_halves[0])
-        later = [(prepare_x, (n,), False) for n in x_pairs[1:]]
-        later += [(prepare_w, h, True) for h in w_halves[1:]]
-        assert len(later) == HALVES * TILE_PAIRS
-        v_result = [results.tile([P, WIDTH], F32, name="result") for t in range(TOKEN_TILES)]
-        for a in range(HALVES):
-            for n in x_pairs:
-                step = a * TILE_PAIRS + n
-                if step + 1 < len(later) and later[step + 1][2]:
-                    sort_w(*later[step + 1][1])
-                prepare, piece, to_sort = later[step]
-                prepare(*piece)
-                for t in (2 * n, 2 * n + 1):
-                    leave_whole(project_half(V, a, t, v_result[t]), a, v_result[t])
-                    if a == HALVES - 1:
-                        store(V, t, v_result[t])
-
         waiting = []
 
         def finish_waiting():
@@ -314,15 +296,69 @@ def tile_progenattention_pa_kernel(tc, hidden_states, W_qkv, out_0, out_1, out_2
                 store(s, t, result)
             waiting.clear()
 
-        for s in (Q, K):
-            for t in range(TOKEN_TILES):
-                result = results.tile([P, WIDTH], F32, name="result")
-                products = stage.tile([P, 2, HEADS, ROT], F32, name="products")
-                for a in range(HALVES):
-                    sums = project_half(s, a, t, result)
-                    leave_unrotated(sums, a, result)
-                    rotation_products(sums, t, a, products)
-                    if a == 0:
-                        finish_waiting()
-                waiting.append((s, t, result, products))
+        def rotated_tile(s, t):
+            result = results.tile([P, WIDTH], F32, name="result")
+            products = stage.tile([P, 2, HEADS, ROT], F32, name="products")
+            for a in range(HALVES):
+                sums = project_half(s, a, t)
+                rotation_products(sums, t, a, products)
+                nc.scalar.copy(
+                    out=by_head(result[:, a * HALF : (a + 1) * HALF])[:, :, ROT:DH],
+                    in_=by_head(sums[:])[:, :, ROT:DH],
+                )
+                if a == 0:
+                    finish_waiting()
+            waiting.append((s, t, result, products))
+
+        transpose_x(0)
+        transpose_w(V, 0, 1)
+        quantise_x(0)
+        transpose_w(V, 1, 1)
+        quantise_w(V, 0)
+        v_half(0, 0)
+        v_half(0, 1)
+        quantise_w(V, 1)
+        sort_piece(("x", 2))
+        transpose_x(1)
+        v_half(1, 0)
+        v_half(1, 1)
+        quantise_x(1)
+        transpose_x(2)
+        sort_piece(("x", 3))
+        sort_piece((Q, 0))
+        sort_piece((Q, 1))
+        for t in (2, 3):
+            for a in range(HALVES):
+                v_half(a, t)
+        quantise_x(2)
+        transpose_x(3)
+        transpose_w(Q, 0, 1)
+        sort_piece((Q, 2))
+        sort_piece((Q, 3))
+        for t in (4, 5):
+            for a in range(HALVES):
+                v_half(a, t)
+        quantise_x(3)
+        quantise_w(Q, 0)
+        transpose_w(Q, 1, 1)
+        sort_piece((K, 0))
+        sort_piece((K, 1))
+        for t in (6, 7):
+            for a in range(HALVES):
+                v_half(a, t)
+        quantise_w(Q, 1)
+        transpose_w(K, 0, 0)
+        sort_piece((K, 2))
+        sort_piece((K, 3))
+        rotated_tile(Q, 0)
+        rotated_tile(Q, 1)
+        quantise_w(K, 0)
+        transpose_w(K, 1, 0)
+        rotated_tile(Q, 2)
+        rotated_tile(Q, 3)
+        quantise_w(K, 1)
+        for t in range(4, TOKEN_TILES):
+            rotated_tile(Q, t)
+        for t in range(TOKEN_TILES):
+            rotated_tile(K, t)
         finish_waiting()

@@ -143,9 +143,9 @@ def tile_progenattention_pa_kernel(tc, hidden_states, W_qkv, out_0, out_1, out_2
             for a in range(HALVES):
                 load_w(s, a)
 
+        table = build_rope_tables(nc, consts)
         identity = consts.tile([P, P], F32, name="identity")
         make_identity(nc, identity[:])
-        table = build_rope_tables(nc, consts)
 
         VECTOR, SCALAR = 0, 1
 
@@ -313,7 +313,7 @@ def tile_progenattention_pa_kernel(tc, hidden_states, W_qkv, out_0, out_1, out_2
         transpose_x(0)
         transpose_w(V, 0, 1)
         quantise_x(0)
-        transpose_w(V, 1, 1)
+        transpose_w(V, 1, 0)
         quantise_w(V, 0)
         v_half(0, 0)
         v_half(0, 1)

@@ -179,7 +179,7 @@ def tile_progenattention_pa_kernel(tc, hidden_states, W_qkv, out_0, out_1, out_2
         x_scales = keep.tile([P, TOKEN_TILES * PASSES * P], U8, name="x_scales", align_bytes=64)
         grouped = {}
 
-        def transpose_x(n):
+        def transpose_x(n, engines=(VECTOR, SCALAR)):
             x_grouped = stage.tile(
                 [P, 2, PASSES * P * 4], BF16, name="x_grouped", tag="grouped", align_bytes=64
             )
@@ -189,7 +189,7 @@ def tile_progenattention_pa_kernel(tc, hidden_states, W_qkv, out_0, out_1, out_2
                     for u in range(2):
                         transpose_words(x_bank[:, 2 * c + u, :], ("x", n), i, c, u)
                 leave_psum(
-                    (VECTOR, SCALAR)[i],
+                    engines[i],
                     x_grouped[:, i, :].bitcast(F32).rearrange("q (c p u) -> q c p u", c=PASSES, u=2),
                     x_bank[:].rearrange("q (c u) p -> q c p u", u=2),
                 )
@@ -313,13 +313,13 @@ def tile_progenattention_pa_kernel(tc, hidden_states, W_qkv, out_0, out_1, out_2
         transpose_x(0)
         transpose_w(V, 0, 1)
         quantise_x(0)
-        transpose_w(V, 1, 0)
+        transpose_w(V, 1, 1)
         quantise_w(V, 0)
-        v_half(0, 0)
-        v_half(0, 1)
+        transpose_x(1, (SCALAR, SCALAR))
         quantise_w(V, 1)
         sort_piece(("x", 2))
-        transpose_x(1)
+        v_half(0, 0)
+        v_half(0, 1)
         v_half(1, 0)
         v_half(1, 1)
         quantise_x(1)

@@ -175,8 +175,8 @@ def tile_progenattention_pa_kernel(tc, hidden_states, W_qkv, out_0, out_1, out_2
                 chosen = words[:, first + u : first + 2 * P : 2]
             nc.tensor.transpose(out=out, in_=chosen, identity=identity[:])
 
-        x_codes = keep.tile([P, TOKEN_TILES * PASSES * P], U32, name="x_codes", align_bytes=64)
-        x_scales = keep.tile([P, TOKEN_TILES * PASSES * P], U8, name="x_scales", align_bytes=64)
+        x_codes = keep.tile([P, TOKEN_TILES * PASSES * P], U32, name="x_codes", align_bytes=256)
+        x_scales = keep.tile([P, TOKEN_TILES * PASSES * P], U8, name="x_scales", align_bytes=256)
         grouped = {}
 
         def transpose_x(n, engines=(VECTOR, SCALAR)):
@@ -207,10 +207,10 @@ def tile_progenattention_pa_kernel(tc, hidden_states, W_qkv, out_0, out_1, out_2
         w_scales = {}
         for s in (V, Q, K):
             w_codes[s] = keep.tile(
-                [P, HALVES, PASSES, HALF], U32, name="w_codes_%d" % s, align_bytes=64
+                [P, HALVES, PASSES, HALF], U32, name="w_codes_%d" % s, align_bytes=256
             )
             w_scales[s] = keep.tile(
-                [P, HALVES, PASSES, HALF], U8, name="w_scales_%d" % s, align_bytes=64
+                [P, HALVES, PASSES, HALF], U8, name="w_scales_%d" % s, align_bytes=256
             )
 
         def transpose_w(s, a, vector_banks):

import math
from contextlib import ExitStack

import concourse.mybir as mybir
from concourse.masks import make_identity

F32 = mybir.dt.float32
BF16 = mybir.dt.bfloat16
I32 = mybir.dt.int32
U32 = mybir.dt.uint32
U8 = mybir.dt.uint8
FP8X4 = mybir.dt.float8_e4m3fn_x4
ALU = mybir.AluOpType
ACT = mybir.ActivationFunctionType

P = 128
SEQ = 512
TOKENS = 2 * SEQ
TOKEN_TILES = TOKENS // P
TILE_PAIRS = TOKEN_TILES // 2
E = 1024
PASSES = E // 512
HEADS = 8
DH = 128
ROT = 32
PAIRS = ROT // 2
WIDTH = HEADS * DH
GROUPS = 4
GROUP_ROWS = WIDTH // GROUPS
HALVES = 2
HALF = WIDTH // HALVES
Q, K, V = 0, 1, 2
PSUM_BANKS = 8

FLOPS = 2 * TOKENS * E * 3 * WIDTH

ROUND_MAGIC = 1.5 * 2.0**23
TURN_HI = 6.28125
TURN_LO = 2.0 * math.pi - TURN_HI


def build_rope_tables(nc, pool):
    token = pool.tile([P, TOKEN_TILES], I32, name="token")
    nc.gpsimd.iota(token[:], pattern=[[1, TOKEN_TILES]], base=0, channel_multiplier=TOKEN_TILES)
    position_i = pool.tile([P, TOKEN_TILES], I32, name="position_i")
    nc.vector.tensor_single_scalar(out=position_i[:], in_=token[:], scalar=SEQ - 1, op=ALU.bitwise_and)
    position = pool.tile([P, TOKEN_TILES], F32, name="position")
    nc.vector.tensor_copy(out=position[:], in_=position_i[:])

    shape = [P, TOKEN_TILES, PAIRS]
    angle = pool.tile(shape, F32, name="angle")
    for j in range(PAIRS):
        nc.vector.tensor_scalar_mul(
            out=angle[:, :, j], in0=position[:], scalar1=10000.0 ** (-2.0 * j / ROT)
        )
    turns = pool.tile(shape, F32, name="turns")
    nc.vector.tensor_scalar(
        out=turns[:], in0=angle[:], scalar1=0.5 / math.pi, scalar2=ROUND_MAGIC,
        op0=ALU.mult, op1=ALU.add,
    )
    nc.vector.tensor_scalar_sub(out=turns[:], in0=turns[:], scalar1=ROUND_MAGIC)
    partly = pool.tile(shape, F32, name="partly")
    nc.vector.scalar_tensor_tensor(
        out=partly[:], in0=turns[:], scalar=-TURN_HI, in1=angle[:], op0=ALU.mult, op1=ALU.add
    )
    reduced = pool.tile(shape, F32, name="reduced")
    nc.vector.scalar_tensor_tensor(
        out=reduced[:], in0=turns[:], scalar=-TURN_LO, in1=partly[:], op0=ALU.mult, op1=ALU.add
    )
    sin_half = pool.tile(shape, F32, name="sin_half")
    nc.scalar.activation(out=sin_half[:], in_=reduced[:], func=ACT.Sin, scale=0.5)
    size = pool.tile(shape, F32, name="size")
    nc.vector.scalar_tensor_tensor(
        out=size[:], in0=reduced[:], scalar=-1.0, in1=reduced[:], op0=ALU.mult, op1=ALU.max
    )
    nc.vector.tensor_scalar(
        out=size[:], in0=size[:], scalar1=-0.5, scalar2=0.5 * math.pi, op0=ALU.mult, op1=ALU.add
    )
    cos_half = pool.tile(shape, F32, name="cos_half")
    nc.scalar.activation(out=cos_half[:], in_=size[:], func=ACT.Sin)

    table = pool.tile([P, TOKEN_TILES, 2, ROT], F32, name="table")
    entry = table[:].rearrange("p t r (j c) -> p t r j c", c=2)
    nc.vector.scalar_tensor_tensor(
        out=entry[:, :, 1, :, 0], in0=sin_half[:], scalar=2.0, in1=cos_half[:],
        op0=ALU.mult, op1=ALU.mult,
    )
    nc.vector.scalar_tensor_tensor(
        out=entry[:, :, 0, :, 1], in0=sin_half[:], scalar=-2.0, in1=cos_half[:],
        op0=ALU.mult, op1=ALU.mult,
    )
    cos_less_1 = pool.tile(shape, F32, name="cos_less_1")
    nc.vector.scalar_tensor_tensor(
        out=cos_less_1[:], in0=sin_half[:], scalar=-2.0, in1=sin_half[:],
        op0=ALU.mult, op1=ALU.mult,
    )
    nc.vector.tensor_scalar_add(out=entry[:, :, 0, :, 0], in0=cos_less_1[:], scalar1=1.0)
    nc.vector.tensor_scalar_add(out=entry[:, :, 1, :, 1], in0=cos_less_1[:], scalar1=1.0)
    return table


def tile_progenattention_pa_kernel(tc, hidden_states, W_qkv, out_0, out_1, out_2):
    nc = tc.nc

    x_dram = hidden_states.rearrange("b s k -> (b s) k").rearrange(
        "(p t) k -> p t k", t=TOKEN_TILES
    )
    out_dram = [
        out.rearrange("b s h d -> (b s) (h d)").rearrange("(p t) c -> p t c", t=TOKEN_TILES)
        for out in (out_0, out_1, out_2)
    ]
    w_dram = W_qkv.rearrange("(g s p i) k -> s g p (i k)", g=GROUPS, s=3, p=P, i=2)

    with ExitStack() as ctx:
        consts = ctx.enter_context(tc.tile_pool(name="consts", bufs=1))
        raw = ctx.enter_context(tc.tile_pool(name="raw", bufs=1))
        keep = ctx.enter_context(tc.tile_pool(name="keep", bufs=1))
        stage = ctx.enter_context(tc.tile_pool(name="stage", bufs=4))
        results = ctx.enter_context(tc.tile_pool(name="results", bufs=12))
        psum = ctx.enter_context(tc.psum_pool(name="psum", bufs=PSUM_BANKS))
        ctx.enter_context(tc.manual_schedule())

        pieces = {}

        def load_x(n):
            pieces[("x", n)] = raw.tile([P, 2 * E], BF16, name="x_raw_%d" % n)
            nc.sync.dma_start(
                out=pieces[("x", n)][:].rearrange("p (i k) -> p i k", i=2),
                in_=x_dram[:, 2 * n : 2 * n + 2, :],
            )

        def load_w(s, a):
            for g in (2 * a, 2 * a + 1):
                pieces[(s, g)] = raw.tile([P, 2 * E], BF16, name="w_raw_%d_%d" % (s, g))
                nc.sync.dma_start(out=pieces[(s, g)][:], in_=w_dram[s, g, :, :])

        load_x(0)
        load_w(V, 0)
        load_w(V, 1)
        for n in range(1, TILE_PAIRS):
            load_x(n)
        for s in (Q, K):
            for a in range(HALVES):
                load_w(s, a)

        table = build_rope_tables(nc, consts)
        identity = consts.tile([P, P], F32, name="identity")
        make_identity(nc, identity[:])

        VECTOR, SCALAR = 0, 1

        def leave_psum(engine, out, in_):
            if engine == VECTOR:
                nc.vector.tensor_copy(out=out, in_=in_)
            else:
                nc.scalar.copy(out=out, in_=in_)

        is_sorted = set()

        def sort_piece(key):
            tidy = stage.tile([P, 2 * E], BF16, name="tidy")
            nc.vector.tensor_copy(
                out=tidy[:].bitcast(F32).rearrange("q (b u p) -> q b u p", u=2, p=P),
                in_=pieces[key][:].bitcast(F32).rearrange("q (b p u) -> q b u p", u=2, p=P),
            )
            pieces[key] = tidy
            is_sorted.add(key)

        def transpose_words(out, key, i, c, u):
            words = pieces[key][:].bitcast(F32)
            first = (2 * i + c) * 2 * P
            if key in is_sorted:
                chosen = words[:, first + u * P : first + (u + 1) * P]
            else:
                chosen = words[:, first + u : first + 2 * P : 2]
            nc.tensor.transpose(out=out, in_=chosen, identity=identity[:])

        x_codes = keep.tile([P, TOKEN_TILES * PASSES * P], U32, name="x_codes", align_bytes=256)
        x_scales = keep.tile([P, TOKEN_TILES * PASSES * P], U8, name="x_scales", align_bytes=256)
        grouped = {}

        def transpose_x(n, engines=(VECTOR, SCALAR)):
            x_grouped = stage.tile(
                [P, 2, PASSES * P * 4], BF16, name="x_grouped", tag="grouped", align_bytes=64
            )
            for i in range(2):
                x_bank = psum.tile([P, 4, P], F32, name="x_bank", tag="bank")
                for c in range(PASSES):
                    for u in range(2):
                        transpose_words(x_bank[:, 2 * c + u, :], ("x", n), i, c, u)
                leave_psum(
                    engines[i],
                    x_grouped[:, i, :].bitcast(F32).rearrange("q (c p u) -> q c p u", c=PASSES, u=2),
                    x_bank[:].rearrange("q (c u) p -> q c p u", u=2),
                )
            grouped[("x", n)] = x_grouped

        def quantise_x(n):
            both_tiles = slice(2 * n * PASSES * P, 2 * (n + 1) * PASSES * P)
            nc.vector.quantize_mx(
                out=x_codes[:, both_tiles].bitcast(FP8X4),
                scales=x_scales[:, both_tiles],
                in_=grouped[("x", n)][:].rearrange("q i k -> q (i k)"),
            )

        w_codes = {}
        w_scales = {}
        for s in (V, Q, K):
            w_codes[s] = keep.tile(
                [P, HALVES, PASSES, HALF], U32, name="w_codes_%d" % s, align_bytes=256
            )
            w_scales[s] = keep.tile(
                [P, HALVES, PASSES, HALF], U8, name="w_scales_%d" % s, align_bytes=256
            )

        def transpose_w(s, a, vector_banks):
            w_grouped = stage.tile(
                [P, PASSES, HALF * 4], BF16, name="w_grouped", tag="grouped", align_bytes=64
            )
            for g in range(2):
                for c in range(PASSES):
                    w_bank = psum.tile([P, 4, P], F32, name="w_bank", tag="bank")
                    for i in range(2):
                        for u in range(2):
                            transpose_words(w_bank[:, 2 * i + u, :], (s, 2 * a + g), i, c, u)
                    group = w_grouped[:, c, g * 4 * GROUP_ROWS : (g + 1) * 4 * GROUP_ROWS]
                    leave_psum(
                        VECTOR if 2 * g + c < vector_banks else SCALAR,
                        group.bitcast(F32).rearrange("q (p b) -> q p b", b=4),
                        w_bank[:].rearrange("q b p -> q p b"),
                    )
            grouped[(s, a)] = w_grouped

        def quantise_w(s, a):
            nc.vector.quantize_mx(
                out=w_codes[s][:, a, :, :].rearrange("q c n -> q (c n)").bitcast(FP8X4),
                scales=w_scales[s][:, a, :, :].rearrange("q c n -> q (c n)"),
                in_=grouped[(s, a)][:].rearrange("q c k -> q (c k)"),
            )

        def project_half(s, a, t):
            sums = psum.tile([P, HALF], F32, name="sums", tag="bank")
            for c in range(PASSES):
                tokens = slice((PASSES * t + c) * P, (PASSES * t + c + 1) * P)
                nc.tensor.matmul_mx(
                    out=sums[:],
                    lhsT=x_codes[:, tokens].bitcast(FP8X4),
                    lhsT_scale=x_scales[:, tokens],
                    rhs=w_codes[s][:, a, c, :].bitcast(FP8X4),
                    rhs_scale=w_scales[s][:, a, c, :],
                    start=(c == 0),
                    stop=(c == PASSES - 1),
                )
            return sums

        def by_head(columns):
            return columns.rearrange("p (h d) -> p h d", d=DH)

        def store(s, t, result):
            nc.sync.dma_start(out=out_dram[s][:, t, :], in_=result[:])

        v_result = {}

        def v_half(a, t):
            if a == 0:
                v_result[t] = results.tile([P, WIDTH], F32, name="result")
            sums = project_half(V, a, t)
            nc.scalar.copy(out=v_result[t][:, a * HALF : (a + 1) * HALF], in_=sums[:])
            if a == HALVES - 1:
                store(V, t, v_result[t])

        def rotation_products(sums, t, a, products):
            heads = HEADS // HALVES
            shape = [P, 2, heads, ROT]
            nc.vector.tensor_tensor(
                out=products[:, :, a * heads : (a + 1) * heads, :],
                in0=by_head(sums[:])[:, :, 0:ROT].unsqueeze(1).to_broadcast(shape),
                in1=table[:, t, :, :].unsqueeze(2).to_broadcast(shape),
                op=ALU.mult,
            )

        def rotation_sums(result, products):
            terms = products[:].rearrange("p r h (j c) -> p h j r c", c=2)
            nc.vector.tensor_tensor(
                out=by_head(result[:])[:, :, 0:ROT].rearrange("p h (j r) -> p h j r", r=2),
                in0=terms[:, :, :, :, 0],
                in1=terms[:, :, :, :, 1],
                op=ALU.add,
            )

        waiting = []

        def finish_waiting():
            for s, t, result, products in waiting:
                rotation_sums(result, products)
                store(s, t, result)
            waiting.clear()

        def rotated_tile(s, t):
            result = results.tile([P, WIDTH], F32, name="result")
            products = stage.tile([P, 2, HEADS, ROT], F32, name="products")
            for a in range(HALVES):
                sums = project_half(s, a, t)
                rotation_products(sums, t, a, products)
                nc.scalar.copy(
                    out=by_head(result[:, a * HALF : (a + 1) * HALF])[:, :, ROT:DH],
                    in_=by_head(sums[:])[:, :, ROT:DH],
                )
                if a == 0:
                    finish_waiting()
            waiting.append((s, t, result, products))

        transpose_x(0)
        transpose_w(V, 0, 1)
        quantise_x(0)
        transpose_w(V, 1, 1)
        quantise_w(V, 0)
        transpose_x(1, (SCALAR, SCALAR))
        quantise_w(V, 1)
        sort_piece(("x", 2))
        v_half(0, 0)
        v_half(0, 1)
        v_half(1, 0)
        v_half(1, 1)
        quantise_x(1)
        transpose_x(2)
        sort_piece(("x", 3))
        sort_piece((Q, 0))
        sort_piece((Q, 1))
        for t in (2, 3):
            for a in range(HALVES):
                v_half(a, t)
        quantise_x(2)
        transpose_x(3)
        transpose_w(Q, 0, 1)
        sort_piece((Q, 2))
        sort_piece((Q, 3))
        for t in (4, 5):
            for a in range(HALVES):
                v_half(a, t)
        quantise_x(3)
        quantise_w(Q, 0)
        transpose_w(Q, 1, 1)
        sort_piece((K, 0))
        sort_piece((K, 1))
        for t in (6, 7):
            for a in range(HALVES):
                v_half(a, t)
        quantise_w(Q, 1)
        transpose_w(K, 0, 0)
        sort_piece((K, 2))
        sort_piece((K, 3))
        rotated_tile(Q, 0)
        rotated_tile(Q, 1)
        quantise_w(K, 0)
        transpose_w(K, 1, 0)
        rotated_tile(Q, 2)
        rotated_tile(Q, 3)
        quantise_w(K, 1)
        for t in range(4, TOKEN_TILES):
            rotated_tile(Q, t)
        for t in range(TOKEN_TILES):
            rotated_tile(K, t)
        finish_waiting()
